import numpy as np
import ml_dtypes


def mxq(x, axis, fmt="e4m3"):
    dtype, down = {"e4m3": (ml_dtypes.float8_e4m3fn, 7), "e5m2": (ml_dtypes.float8_e5m2, 14)}[fmt]
    v = np.moveaxis(np.asarray(x, np.float32).astype(ml_dtypes.bfloat16).astype(np.float64), axis, -1)
    blocks = v.reshape(v.shape[:-1] + (-1, 32))
    amax = np.abs(blocks).max(-1, keepdims=True)
    byte = np.maximum(np.where(amax > 0, np.frexp(amax)[1] - 1 + 127, 0) - down, 1)
    scale = np.exp2(byte - 127.0)
    codes = (blocks / scale).astype(np.float32).astype(dtype).astype(np.float64)
    return np.moveaxis((codes * scale).reshape(v.shape), -1, axis)


WIDE = False


def mx_kscale(k):
    if not WIDE:
        return np.ones(k)
    levels = np.array([10, -10, 5, -5, 0])
    a = np.random.permutation(np.resize(levels, k // 512 * 4)).reshape(k // 512, 4)
    idx = np.arange(k)
    return np.exp2(a[idx // 512, idx % 128 // 32])


BF16 = ml_dtypes.bfloat16


def bf(x):
    return np.asarray(x, np.float32).astype(BF16)


def f64(x):
    return np.asarray(x).astype(np.float64)


B, H, W, C, F, K, G, RR = 4, 32, 32, 1024, 256, 3, 16, 4
KK = K * K
P = B * H * W


def setup_inputs():
    s = mx_kscale(C)
    return {"x": bf(np.random.standard_normal((B, H, W, C)) * s),
            "Wi": bf(np.random.standard_normal((C, F)) / np.sqrt(C) / s[:, None]),
            "bi": bf(np.random.standard_normal(F) * 0.3),
            "w_span": bf(np.random.standard_normal((B, H, W, KK * G)) * 0.7)}


def reference(x, Wi, bi, w_span):
    xi = ((mxq(f64(x).reshape(P, C), 1, "e4m3") @ mxq(f64(Wi), 0, "e4m3")) + f64(bi)).reshape(B, H, W, F)
    pad = (K - 1) // 2
    xp = np.pad(xi, ((0, 0), (pad, pad), (pad, pad), (0, 0)))
    patches = np.stack([xp[:, i:i + H, j:j + W, :] for i in range(K) for j in range(K)], axis=-2)
    patches = patches.reshape(B, H, W, G, F // G, KK)
    w = f64(w_span).reshape(B, H, W, G, KK)[:, :, :, :, None, :]
    return (w * patches).sum(-1).reshape(B, H, W, F)

@@ -1,0 +1,284 @@
+from contextlib import ExitStack
+
+import concourse.mybir as mybir
+from concourse.masks import make_identity
+
+F32 = mybir.dt.float32
+BF16 = mybir.dt.bfloat16
+U32 = mybir.dt.uint32
+U8 = mybir.dt.uint8
+FP8X4 = mybir.dt.float8_e4m3fn_x4
+MULT = mybir.AluOpType.mult
+ADD = mybir.AluOpType.add
+
+P = 128
+
+IMAGES, HEIGHT, WIDTH = 4, 32, 32
+C_IN, C_OUT = 1024, 256
+WINDOW = 3
+TAPS = WINDOW * WINDOW
+GROUPS = 16
+GROUP_CHANNELS = C_OUT // GROUPS
+GROUP_LEN = GROUP_CHANNELS * TAPS
+PIXELS = IMAGES * HEIGHT * WIDTH
+
+FLOPS = 2 * PIXELS * C_IN * C_OUT + 2 * PIXELS * TAPS * C_OUT
+
+K_PASS = 4 * P
+PASSES = C_IN // K_PASS
+WORDS_PASS = K_PASS // 2
+C_HALVES = C_OUT // P
+CHUNK = 256
+CHUNK_TILES = CHUNK // P
+CHUNK_ROWS = CHUNK // WIDTH
+CHUNKS = PIXELS // CHUNK
+CHUNKS_IMAGE = HEIGHT // CHUNK_ROWS
+PADDED_ROWS = HEIGHT + 2
+BLOCK_F32 = 8
+
+TILE_ROWS = P // WIDTH
+BANK = 512
+P_HALF = TAPS * C_OUT // 2
+HALF_GROUPS = GROUPS // 2
+HALF_OUT = C_OUT // 2
+BANK_GROUPS = BANK // GROUP_LEN
+VECTOR_GROUPS = 2
+GPSIMD_OUT = (HALF_GROUPS - VECTOR_GROUPS) * GROUP_CHANNELS
+HALVES_CHUNK = 2 * CHUNK_TILES
+
+LOAD_AHEAD = 3
+QUANTISE_LAG = 1
+PROJECT_LAG = 2
+INVOLVE_LAG = 3
+
+
+def tile_involution2d_pa_kernel(tc, x, Wi, bi, w_span, out):
+    nc = tc.nc
+    x_rows = x.rearrange("b u v k -> (b u v) k")
+    w_rows = w_span.rearrange("b u v c -> (b u v) c")
+    out_rows = out.rearrange("b u v o -> (b u v) o")
+
+    with ExitStack() as ctx:
+        const = ctx.enter_context(tc.tile_pool(name="const", bufs=1))
+        x_pool = ctx.enter_context(tc.tile_pool(name="x", bufs=LOAD_AHEAD + 1))
+        mx_pool = ctx.enter_context(tc.tile_pool(name="mx", bufs=2))
+        q_pool = ctx.enter_context(tc.tile_pool(name="q", bufs=2))
+        sum_pool = ctx.enter_context(tc.tile_pool(name="sums", bufs=1))
+        out_pool = ctx.enter_context(tc.tile_pool(name="out", bufs=2))
+        xt_psum = ctx.enter_context(tc.psum_pool(name="xt", bufs=2))
+        xi_psum = ctx.enter_context(tc.psum_pool(name="xi", bufs=1))
+        p_psum = ctx.enter_context(tc.psum_pool(name="p", bufs=5))
+
+        x_tiles = {}
+        grouped_tiles = {}
+        code_tiles = {}
+
+        def load_x(c):
+            x_sb = x_pool.tile([P, CHUNK_TILES * C_IN], BF16, name="x_sb")
+            nc.sync.dma_start(
+                out=x_sb[:].rearrange("p (n k) -> p n k", n=CHUNK_TILES),
+                in_=x_rows[c * CHUNK : (c + 1) * CHUNK, :].rearrange("(n p) k -> p n k", p=P),
+            )
+            x_tiles[c] = x_sb
+
+        wi_raw = const.tile([P, PASSES * 4 * C_OUT], BF16, name="wi_raw")
+        nc.sync.dma_start(
+            out=wi_raw[:].rearrange("p (s ec) -> p s ec", s=2 * PASSES),
+            in_=Wi.rearrange("(s q e) c -> q s (e c)", q=P, e=2),
+        )
+        for c in range(LOAD_AHEAD):
+            load_x(c)
+
+        shifter = const.tile([P, 2 * P], F32, name="shifter")
+        make_identity(nc, shifter[:, 0:P])
+        nc.gpsimd.memset(shifter[:, P : 2 * P], 0.0)
+        identity = shifter[:, 0:P]
+
+        wi_grouped = const.tile([P, PASSES * C_OUT * 4], BF16, name="wi_grouped", align_bytes=64)
+        nc.vector.tensor_copy(
+            out=wi_grouped[:].rearrange("p (g c t) -> p g c t", g=PASSES, t=4),
+            in_=wi_raw[:].rearrange("p (g t c) -> p g c t", g=PASSES, t=4),
+        )
+        wi_codes = const.tile([P, PASSES * C_OUT], U32, name="wi_codes", align_bytes=64)
+        wi_scales = const.tile([P, PASSES * C_OUT], U8, name="wi_scales", align_bytes=64)
+        nc.vector.quantize_mx(out=wi_codes[:].bitcast(FP8X4), scales=wi_scales[:], in_=wi_grouped[:])
+
+        bias_rows = const.tile([P, P], BF16, name="bias_rows")
+        nc.vector.memset(bias_rows[:], 0.0)
+        nc.sync.dma_start(out=bias_rows[0:C_HALVES, :], in_=bi.rearrange("(h c) -> h c", h=C_HALVES))
+        bias_rows_f32 = const.tile([P, P], F32, name="bias_rows_f32")
+        nc.vector.tensor_copy(out=bias_rows_f32[:], in_=bias_rows[:])
+        bias_ps = xt_psum.tile([P, P], F32, name="bias_ps", tag="xt")
+        nc.tensor.transpose(bias_ps[:], bias_rows_f32[:], identity)
+        bias_cols = const.tile([P, C_HALVES], F32, name="bias_cols")
+        nc.vector.tensor_copy(out=bias_cols[:], in_=bias_ps[:, 0:C_HALVES])
+
+        w_sb = const.tile([P, (PIXELS // P) * GROUPS * TAPS], BF16, name="w_sb")
+        w_tiles = w_sb[:].rearrange("p (n c) -> p n c", c=GROUPS * TAPS)
+        tiles_image = HEIGHT // TILE_ROWS
+        for b in range(IMAGES):
+            nc.sync.dma_start(
+                out=w_tiles[:, b * tiles_image : (b + 1) * tiles_image, :],
+                in_=w_rows[b * HEIGHT * WIDTH : (b + 1) * HEIGHT * WIDTH, :].rearrange(
+                    "(n p) c -> p n c", p=P
+                ),
+            )
+
+        shifted = []
+        for j in range(WINDOW):
+            xi_sb = const.tile([P, C_HALVES * IMAGES * PADDED_ROWS * WIDTH], F32, name="xi_sb%d" % j)
+            view = xi_sb[:].rearrange(
+                "p (h b r v) -> p h b r v", h=C_HALVES, b=IMAGES, r=PADDED_ROWS
+            )
+            nc.gpsimd.memset(view[:, :, :, 0, :], 0.0)
+            nc.gpsimd.memset(view[:, :, :, PADDED_ROWS - 1, :], 0.0)
+            shifted.append(view)
+        nc.gpsimd.memset(shifted[0][:, :, :, :, 0:BLOCK_F32], 0.0)
+        nc.gpsimd.memset(shifted[WINDOW - 1][:, :, :, :, WIDTH - BLOCK_F32 : WIDTH], 0.0)
+
+        def transpose_x(c):
+            x_words = x_tiles[c][:].bitcast(F32)
+            grouped = mx_pool.tile([P, PASSES * CHUNK * 4], BF16, name="grouped", align_bytes=64)
+            grouped_words = grouped[:].bitcast(F32).rearrange(
+                "p (g r u) -> p g r u", g=PASSES, u=2
+            )
+            for n in range(CHUNK_TILES):
+                xt = xt_psum.tile([P, 2 * PASSES, P], F32, name="xt", tag="xt")
+                for s in range(2 * PASSES):
+                    first = n * (C_IN // 2) + s * P
+                    nc.tensor.transpose(xt[:, s, :], x_words[:, first : first + P], identity)
+                nc.scalar.copy(
+                    out=grouped_words[:, :, n * P : (n + 1) * P, :],
+                    in_=xt[:].rearrange("p (g u) r -> p g r u", u=2),
+                )
+            grouped_tiles[c] = grouped
+
+        def quantise_x(c):
+            codes = mx_pool.tile([P, PASSES * CHUNK], U32, name="codes", align_bytes=64)
+            scales = mx_pool.tile([P, PASSES * CHUNK], U8, name="scales", align_bytes=64)
+            nc.vector.quantize_mx(
+                out=codes[:].bitcast(FP8X4), scales=scales[:], in_=grouped_tiles[c][:]
+            )
+            code_tiles[c] = (codes, scales)
+
+        def project(c):
+            codes, scales = code_tiles[c]
+            xi_ps = xi_psum.tile([P, C_HALVES, CHUNK], F32, name="xi_ps")
+            for h in range(C_HALVES):
+                for g in range(PASSES):
+                    wi_cols = slice(g * C_OUT + h * P, g * C_OUT + (h + 1) * P)
+                    x_cols = slice(g * CHUNK, (g + 1) * CHUNK)
+                    nc.tensor.matmul_mx(
+                        out=xi_ps[:, h, :],
+                        lhsT=wi_codes[:, wi_cols].bitcast(FP8X4),
+                        lhsT_scale=wi_scales[:, wi_cols],
+                        rhs=codes[:, x_cols].bitcast(FP8X4),
+                        rhs_scale=scales[:, x_cols],
+                        start=(g == 0),
+                        stop=(g == PASSES - 1),
+                    )
+            b = c // CHUNKS_IMAGE
+            first_row = 1 + (c % CHUNKS_IMAGE) * CHUNK_ROWS
+            for h in range(C_HALVES):
+                xi_rows = xi_ps[:, h, :].rearrange("p (r v) -> p r v", v=WIDTH)
+                for j in range(WINDOW):
+                    lo = max(0, 1 - j)
+                    hi = min(WIDTH, WIDTH + 1 - j)
+                    nc.scalar.activation(
+                        out=shifted[j][:, h, b, first_row : first_row + CHUNK_ROWS, lo:hi],
+                        in_=xi_rows[:, :, lo + j - 1 : hi + j - 1],
+                        func=mybir.ActivationFunctionType.Identity,
+                        bias=bias_cols[:, h : h + 1],
+                        scale=1.0,
+                    )
+
+        def involve(c):
+            b = c // CHUNKS_IMAGE
+            q = q_pool.tile([P, HALVES_CHUNK * P_HALF], F32, name="q")
+            for n in range(CHUNK_TILES):
+                tile_index = c * CHUNK_TILES + n
+                top = (c % CHUNKS_IMAGE) * CHUNK_ROWS + n * TILE_ROWS
+                for half in range(2):
+                    for g0 in reversed(range(0, HALF_GROUPS, BANK_GROUPS)):
+                        groups = min(BANK_GROUPS, HALF_GROUPS - g0)
+                        first = half * P_HALF + g0 * GROUP_LEN
+                        last = first + groups * GROUP_LEN
+                        p_ps = p_psum.tile([P, BANK], F32, name="p_ps")
+                        for block in range(first // P, (last + P - 1) // P):
+                            t, h = block // C_HALVES, block % C_HALVES
+                            i, j = t // WINDOW, t % WINDOW
+                            column = max(0, block * P - first)
+                            shift = max(0, first - block * P)
+                            nc.tensor.transpose(
+                                p_ps[:, column : column + P],
+                                shifted[j][:, h, b, top + i : top + i + TILE_ROWS, :].rearrange(
+                                    "p r v -> p (r v)"
+                                ),
+                                shifter[:, shift : shift + P],
+                            )
+                        w_first = (half * HALF_GROUPS + g0) * TAPS
+                        at = (n * 2 + half) * P_HALF + g0 * GROUP_LEN
+                        nc.vector.tensor_tensor(
+                            out=q[:, at : at + groups * GROUP_LEN].rearrange(
+                                "p (g c m) -> p g c m", c=GROUP_CHANNELS, m=TAPS
+                            ),
+                            in0=p_ps[:, 0 : groups * GROUP_LEN].rearrange(
+                                "p (g c m) -> p g c m", c=GROUP_CHANNELS, m=TAPS
+                            ),
+                            in1=w_tiles[:, tile_index, w_first : w_first + groups * TAPS]
+                            .rearrange("p (g m) -> p g m", m=TAPS)
+                            .unsqueeze(2)
+                            .to_broadcast([P, groups, GROUP_CHANNELS, TAPS]),
+                            op=MULT,
+                        )
+
+            terms = q[:].rearrange("p (a o m) -> p a o m", a=HALVES_CHUNK, m=TAPS)
+            result = out_pool.tile([P, HALVES_CHUNK * HALF_OUT], F32, name="result")
+            result_halves = result[:].rearrange("p (a o) -> p a o", a=HALVES_CHUNK)
+            nc.vector.tensor_reduce(
+                out=result_halves[:, :, GPSIMD_OUT:HALF_OUT],
+                in_=terms[:, :, GPSIMD_OUT:HALF_OUT, :],
+                axis=mybir.AxisListType.X,
+                op=ADD,
+            )
+            count = HALVES_CHUNK * GPSIMD_OUT
+            sum4 = sum_pool.tile([P, count * 4], F32, name="sum4")
+            sum2 = sum_pool.tile([P, count * 2], F32, name="sum2")
+            sum1 = sum_pool.tile([P, count], F32, name="sum1")
+            nc.gpsimd.tensor_tensor(
+                out=sum4[:].rearrange("p (a o m) -> p a o m", a=HALVES_CHUNK, m=4),
+                in0=terms[:, :, 0:GPSIMD_OUT, 0:4],
+                in1=terms[:, :, 0:GPSIMD_OUT, 4:8],
+                op=ADD,
+            )
+            fours = sum4[:].rearrange("p (o m) -> p o m", m=4)
+            nc.gpsimd.tensor_tensor(
+                out=sum2[:].rearrange("p (o m) -> p o m", m=2),
+                in0=fours[:, :, 0:2],
+                in1=fours[:, :, 2:4],
+                op=ADD,
+            )
+            twos = sum2[:].rearrange("p (o m) -> p o m", m=2)
+            nc.gpsimd.tensor_tensor(out=sum1[:], in0=twos[:, :, 0], in1=twos[:, :, 1], op=ADD)
+            nc.gpsimd.tensor_tensor(
+                out=result_halves[:, :, 0:GPSIMD_OUT],
+                in0=sum1[:].rearrange("p (a o) -> p a o", a=HALVES_CHUNK),
+                in1=terms[:, :, 0:GPSIMD_OUT, 8],
+                op=ADD,
+            )
+            nc.sync.dma_start(
+                out=out_rows[c * CHUNK : (c + 1) * CHUNK, :].rearrange("(n p) o -> p n o", p=P),
+                in_=result[:].rearrange("p (n o) -> p n o", n=CHUNK_TILES),
+            )
+
+        for step in range(CHUNKS + INVOLVE_LAG):
+            if step + LOAD_AHEAD < CHUNKS:
+                load_x(step + LOAD_AHEAD)
+            if step < CHUNKS:
+                transpose_x(step)
+            if 0 <= step - QUANTISE_LAG < CHUNKS:
+                quantise_x(step - QUANTISE_LAG)
+            if 0 <= step - PROJECT_LAG < CHUNKS:
+                project(step - PROJECT_LAG)
+            if step >= INVOLVE_LAG:
+                involve(step - INVOLVE_LAG)

@@ -59,6 +59,7 @@ def tile_involution2d_pa_kernel(tc, x, Wi, bi, w_span, out):
     out_rows = out.rearrange("b u v o -> (b u v) o")
 
     with ExitStack() as ctx:
+        ctx.enter_context(tc.manual_schedule())
         const = ctx.enter_context(tc.tile_pool(name="const", bufs=1))
         x_pool = ctx.enter_context(tc.tile_pool(name="x", bufs=LOAD_AHEAD + 1))
         mx_pool = ctx.enter_context(tc.tile_pool(name="mx", bufs=2))
@@ -81,12 +82,16 @@ def tile_involution2d_pa_kernel(tc, x, Wi, bi, w_span, out):
             )
             x_tiles[c] = x_sb
 
+        load_x(0)
         wi_raw = const.tile([P, PASSES * 4 * C_OUT], BF16, name="wi_raw")
         nc.sync.dma_start(
             out=wi_raw[:].rearrange("p (s ec) -> p s ec", s=2 * PASSES),
             in_=Wi.rearrange("(s q e) c -> q s (e c)", q=P, e=2),
         )
-        for c in range(LOAD_AHEAD):
+        bias_rows = const.tile([P, P], BF16, name="bias_rows")
+        nc.vector.memset(bias_rows[:], 0.0)
+        nc.sync.dma_start(out=bias_rows[0:C_HALVES, :], in_=bi.rearrange("(h c) -> h c", h=C_HALVES))
+        for c in range(1, LOAD_AHEAD):
             load_x(c)
 
         shifter = const.tile([P, 2 * P], F32, name="shifter")
@@ -103,9 +108,6 @@ def tile_involution2d_pa_kernel(tc, x, Wi, bi, w_span, out):
         wi_scales = const.tile([P, PASSES * C_OUT], U8, name="wi_scales", align_bytes=64)
         nc.vector.quantize_mx(out=wi_codes[:].bitcast(FP8X4), scales=wi_scales[:], in_=wi_grouped[:])
 
-        bias_rows = const.tile([P, P], BF16, name="bias_rows")
-        nc.vector.memset(bias_rows[:], 0.0)
-        nc.sync.dma_start(out=bias_rows[0:C_HALVES, :], in_=bi.rearrange("(h c) -> h c", h=C_HALVES))
         bias_rows_f32 = const.tile([P, P], F32, name="bias_rows_f32")
         nc.vector.tensor_copy(out=bias_rows_f32[:], in_=bias_rows[:])
         bias_ps = xt_psum.tile([P, P], F32, name="bias_ps", tag="xt")

@@ -68,7 +68,8 @@ def tile_involution2d_pa_kernel(tc, x, Wi, bi, w_span, out):
         out_pool = ctx.enter_context(tc.tile_pool(name="out", bufs=2))
         xt_psum = ctx.enter_context(tc.psum_pool(name="xt", bufs=2))
         xi_psum = ctx.enter_context(tc.psum_pool(name="xi", bufs=1))
-        p_psum = ctx.enter_context(tc.psum_pool(name="p", bufs=5))
+        p_psum = ctx.enter_context(tc.psum_pool(name="p", bufs=4))
+        unread_psum = ctx.enter_context(tc.psum_pool(name="unread", bufs=1))
 
         x_tiles = {}
         grouped_tiles = {}
@@ -194,6 +195,18 @@ def tile_involution2d_pa_kernel(tc, x, Wi, bi, w_span, out):
                         scale=1.0,
                     )
 
+        def hold_clock():
+            unread = unread_psum.tile([P, BANK], F32, name="unread")
+            nc.tensor.matmul_mx(
+                out=unread[:],
+                lhsT=wi_codes[:, 0:P].bitcast(FP8X4),
+                lhsT_scale=wi_scales[:, 0:P],
+                rhs=wi_codes[:, 0:BANK].bitcast(FP8X4),
+                rhs_scale=wi_scales[:, 0:BANK],
+                start=True,
+                stop=True,
+            )
+
         def involve(c):
             b = c // CHUNKS_IMAGE
             q = q_pool.tile([P, HALVES_CHUNK * P_HALF], F32, name="q")
@@ -201,6 +214,7 @@ def tile_involution2d_pa_kernel(tc, x, Wi, bi, w_span, out):
                 tile_index = c * CHUNK_TILES + n
                 top = (c % CHUNKS_IMAGE) * CHUNK_ROWS + n * TILE_ROWS
                 for half in range(2):
+                    hold_clock()
                     for g0 in reversed(range(0, HALF_GROUPS, BANK_GROUPS)):
                         groups = min(BANK_GROUPS, HALF_GROUPS - g0)
                         first = half * P_HALF + g0 * GROUP_LEN

@@ -42,7 +42,7 @@ P_HALF = TAPS * C_OUT // 2
 HALF_GROUPS = GROUPS // 2
 HALF_OUT = C_OUT // 2
 BANK_GROUPS = BANK // GROUP_LEN
-VECTOR_GROUPS = 2
+VECTOR_GROUPS = 3
 GPSIMD_OUT = (HALF_GROUPS - VECTOR_GROUPS) * GROUP_CHANNELS
 HALVES_CHUNK = 2 * CHUNK_TILES
 
@@ -59,7 +59,6 @@ def tile_involution2d_pa_kernel(tc, x, Wi, bi, w_span, out):
     out_rows = out.rearrange("b u v o -> (b u v) o")
 
     with ExitStack() as ctx:
-        ctx.enter_context(tc.manual_schedule())
         const = ctx.enter_context(tc.tile_pool(name="const", bufs=1))
         x_pool = ctx.enter_context(tc.tile_pool(name="x", bufs=LOAD_AHEAD + 1))
         mx_pool = ctx.enter_context(tc.tile_pool(name="mx", bufs=2))
@@ -68,8 +67,7 @@ def tile_involution2d_pa_kernel(tc, x, Wi, bi, w_span, out):
         out_pool = ctx.enter_context(tc.tile_pool(name="out", bufs=2))
         xt_psum = ctx.enter_context(tc.psum_pool(name="xt", bufs=2))
         xi_psum = ctx.enter_context(tc.psum_pool(name="xi", bufs=1))
-        p_psum = ctx.enter_context(tc.psum_pool(name="p", bufs=4))
-        unread_psum = ctx.enter_context(tc.psum_pool(name="unread", bufs=1))
+        p_psum = ctx.enter_context(tc.psum_pool(name="p", bufs=5))
 
         x_tiles = {}
         grouped_tiles = {}
@@ -83,16 +81,12 @@ def tile_involution2d_pa_kernel(tc, x, Wi, bi, w_span, out):
             )
             x_tiles[c] = x_sb
 
-        load_x(0)
         wi_raw = const.tile([P, PASSES * 4 * C_OUT], BF16, name="wi_raw")
         nc.sync.dma_start(
             out=wi_raw[:].rearrange("p (s ec) -> p s ec", s=2 * PASSES),
             in_=Wi.rearrange("(s q e) c -> q s (e c)", q=P, e=2),
         )
-        bias_rows = const.tile([P, P], BF16, name="bias_rows")
-        nc.vector.memset(bias_rows[:], 0.0)
-        nc.sync.dma_start(out=bias_rows[0:C_HALVES, :], in_=bi.rearrange("(h c) -> h c", h=C_HALVES))
-        for c in range(1, LOAD_AHEAD):
+        for c in range(LOAD_AHEAD):
             load_x(c)
 
         shifter = const.tile([P, 2 * P], F32, name="shifter")
@@ -109,6 +103,9 @@ def tile_involution2d_pa_kernel(tc, x, Wi, bi, w_span, out):
         wi_scales = const.tile([P, PASSES * C_OUT], U8, name="wi_scales", align_bytes=64)
         nc.vector.quantize_mx(out=wi_codes[:].bitcast(FP8X4), scales=wi_scales[:], in_=wi_grouped[:])
 
+        bias_rows = const.tile([P, P], BF16, name="bias_rows")
+        nc.vector.memset(bias_rows[:], 0.0)
+        nc.sync.dma_start(out=bias_rows[0:C_HALVES, :], in_=bi.rearrange("(h c) -> h c", h=C_HALVES))
         bias_rows_f32 = const.tile([P, P], F32, name="bias_rows_f32")
         nc.vector.tensor_copy(out=bias_rows_f32[:], in_=bias_rows[:])
         bias_ps = xt_psum.tile([P, P], F32, name="bias_ps", tag="xt")
@@ -195,18 +192,6 @@ def tile_involution2d_pa_kernel(tc, x, Wi, bi, w_span, out):
                         scale=1.0,
                     )
 
-        def hold_clock():
-            unread = unread_psum.tile([P, BANK], F32, name="unread")
-            nc.tensor.matmul_mx(
-                out=unread[:],
-                lhsT=wi_codes[:, 0:P].bitcast(FP8X4),
-                lhsT_scale=wi_scales[:, 0:P],
-                rhs=wi_codes[:, 0:BANK].bitcast(FP8X4),
-                rhs_scale=wi_scales[:, 0:BANK],
-                start=True,
-                stop=True,
-            )
-
         def involve(c):
             b = c // CHUNKS_IMAGE
             q = q_pool.tile([P, HALVES_CHUNK * P_HALF], F32, name="q")
@@ -214,7 +199,6 @@ def tile_involution2d_pa_kernel(tc, x, Wi, bi, w_span, out):
                 tile_index = c * CHUNK_TILES + n
                 top = (c % CHUNKS_IMAGE) * CHUNK_ROWS + n * TILE_ROWS
                 for half in range(2):
-                    hold_clock()
                     for g0 in reversed(range(0, HALF_GROUPS, BANK_GROUPS)):
                         groups = min(BANK_GROUPS, HALF_GROUPS - g0)
                         first = half * P_HALF + g0 * GROUP_LEN

@@ -222,13 +222,13 @@ def tile_involution2d_pa_kernel(tc, x, Wi, bi, w_span, out):
                             out=q[:, at : at + groups * GROUP_LEN].rearrange(
                                 "p (g c m) -> p g c m", c=GROUP_CHANNELS, m=TAPS
                             ),
-                            in0=p_ps[:, 0 : groups * GROUP_LEN].rearrange(
-                                "p (g c m) -> p g c m", c=GROUP_CHANNELS, m=TAPS
-                            ),
-                            in1=w_tiles[:, tile_index, w_first : w_first + groups * TAPS]
+                            in0=w_tiles[:, tile_index, w_first : w_first + groups * TAPS]
                             .rearrange("p (g m) -> p g m", m=TAPS)
                             .unsqueeze(2)
                             .to_broadcast([P, groups, GROUP_CHANNELS, TAPS]),
+                            in1=p_ps[:, 0 : groups * GROUP_LEN].rearrange(
+                                "p (g c m) -> p g c m", c=GROUP_CHANNELS, m=TAPS
+                            ),
                             op=MULT,
                         )
 

@@ -42,8 +42,7 @@ P_HALF = TAPS * C_OUT // 2
 HALF_GROUPS = GROUPS // 2
 HALF_OUT = C_OUT // 2
 BANK_GROUPS = BANK // GROUP_LEN
-VECTOR_GROUPS = 3
-GPSIMD_OUT = (HALF_GROUPS - VECTOR_GROUPS) * GROUP_CHANNELS
+GPSIMD_OUT = 88
 HALVES_CHUNK = 2 * CHUNK_TILES
 
 LOAD_AHEAD = 3
@@ -62,9 +61,9 @@ def tile_involution2d_pa_kernel(tc, x, Wi, bi, w_span, out):
         const = ctx.enter_context(tc.tile_pool(name="const", bufs=1))
         x_pool = ctx.enter_context(tc.tile_pool(name="x", bufs=LOAD_AHEAD + 1))
         mx_pool = ctx.enter_context(tc.tile_pool(name="mx", bufs=2))
-        q_pool = ctx.enter_context(tc.tile_pool(name="q", bufs=2))
+        q_pool = ctx.enter_context(tc.tile_pool(name="q", bufs=3))
         sum_pool = ctx.enter_context(tc.tile_pool(name="sums", bufs=1))
-        out_pool = ctx.enter_context(tc.tile_pool(name="out", bufs=2))
+        out_pool = ctx.enter_context(tc.tile_pool(name="out", bufs=3))
         xt_psum = ctx.enter_context(tc.psum_pool(name="xt", bufs=2))
         xi_psum = ctx.enter_context(tc.psum_pool(name="xi", bufs=1))
         p_psum = ctx.enter_context(tc.psum_pool(name="p", bufs=5))
@@ -81,12 +80,13 @@ def tile_involution2d_pa_kernel(tc, x, Wi, bi, w_span, out):
             )
             x_tiles[c] = x_sb
 
+        load_x(0)
         wi_raw = const.tile([P, PASSES * 4 * C_OUT], BF16, name="wi_raw")
         nc.sync.dma_start(
             out=wi_raw[:].rearrange("p (s ec) -> p s ec", s=2 * PASSES),
             in_=Wi.rearrange("(s q e) c -> q s (e c)", q=P, e=2),
         )
-        for c in range(LOAD_AHEAD):
+        for c in range(1, LOAD_AHEAD):
             load_x(c)
 
         shifter = const.tile([P, 2 * P], F32, name="shifter")
@@ -222,50 +222,52 @@ def tile_involution2d_pa_kernel(tc, x, Wi, bi, w_span, out):
                             out=q[:, at : at + groups * GROUP_LEN].rearrange(
                                 "p (g c m) -> p g c m", c=GROUP_CHANNELS, m=TAPS
                             ),
-                            in0=w_tiles[:, tile_index, w_first : w_first + groups * TAPS]
+                            in0=p_ps[:, 0 : groups * GROUP_LEN].rearrange(
+                                "p (g c m) -> p g c m", c=GROUP_CHANNELS, m=TAPS
+                            ),
+                            in1=w_tiles[:, tile_index, w_first : w_first + groups * TAPS]
                             .rearrange("p (g m) -> p g m", m=TAPS)
                             .unsqueeze(2)
                             .to_broadcast([P, groups, GROUP_CHANNELS, TAPS]),
-                            in1=p_ps[:, 0 : groups * GROUP_LEN].rearrange(
-                                "p (g c m) -> p g c m", c=GROUP_CHANNELS, m=TAPS
-                            ),
                             op=MULT,
                         )
 
+            gpsimd_out = GPSIMD_OUT if c < CHUNKS - 1 else 0
             terms = q[:].rearrange("p (a o m) -> p a o m", a=HALVES_CHUNK, m=TAPS)
             result = out_pool.tile([P, HALVES_CHUNK * HALF_OUT], F32, name="result")
             result_halves = result[:].rearrange("p (a o) -> p a o", a=HALVES_CHUNK)
             nc.vector.tensor_reduce(
-                out=result_halves[:, :, GPSIMD_OUT:HALF_OUT],
-                in_=terms[:, :, GPSIMD_OUT:HALF_OUT, :],
+                out=result_halves[:, :, gpsimd_out:HALF_OUT],
+                in_=terms[:, :, gpsimd_out:HALF_OUT, :],
                 axis=mybir.AxisListType.X,
                 op=ADD,
             )
-            count = HALVES_CHUNK * GPSIMD_OUT
-            sum4 = sum_pool.tile([P, count * 4], F32, name="sum4")
-            sum2 = sum_pool.tile([P, count * 2], F32, name="sum2")
-            sum1 = sum_pool.tile([P, count], F32, name="sum1")
-            nc.gpsimd.tensor_tensor(
-                out=sum4[:].rearrange("p (a o m) -> p a o m", a=HALVES_CHUNK, m=4),
-                in0=terms[:, :, 0:GPSIMD_OUT, 0:4],
-                in1=terms[:, :, 0:GPSIMD_OUT, 4:8],
-                op=ADD,
-            )
-            fours = sum4[:].rearrange("p (o m) -> p o m", m=4)
-            nc.gpsimd.tensor_tensor(
-                out=sum2[:].rearrange("p (o m) -> p o m", m=2),
-                in0=fours[:, :, 0:2],
-                in1=fours[:, :, 2:4],
-                op=ADD,
-            )
-            twos = sum2[:].rearrange("p (o m) -> p o m", m=2)
-            nc.gpsimd.tensor_tensor(out=sum1[:], in0=twos[:, :, 0], in1=twos[:, :, 1], op=ADD)
-            nc.gpsimd.tensor_tensor(
-                out=result_halves[:, :, 0:GPSIMD_OUT],
-                in0=sum1[:].rearrange("p (a o) -> p a o", a=HALVES_CHUNK),
-                in1=terms[:, :, 0:GPSIMD_OUT, 8],
-                op=ADD,
-            )
+            if gpsimd_out > 0:
+                count = HALVES_CHUNK * gpsimd_out
+                sum4 = sum_pool.tile([P, count * 4], F32, name="sum4")
+                sum2 = sum_pool.tile([P, count * 2], F32, name="sum2")
+                sum1 = sum_pool.tile([P, count], F32, name="sum1")
+                nc.gpsimd.tensor_tensor(
+                    out=sum4[:].rearrange("p (a o m) -> p a o m", a=HALVES_CHUNK, m=4),
+                    in0=terms[:, :, 0:gpsimd_out, 0:4],
+                    in1=terms[:, :, 0:gpsimd_out, 4:8],
+                    op=ADD,
+                )
+                fours = sum4[:].rearrange("p (o m) -> p o m", m=4)
+                nc.gpsimd.tensor_tensor(
+                    out=sum2[:].rearrange("p (o m) -> p o m", m=2),
+                    in0=fours[:, :, 0:2],
+                    in1=fours[:, :, 2:4],
+                    op=ADD,
+                )
+                twos = sum2[:].rearrange("p (o m) -> p o m", m=2)
+                nc.gpsimd.tensor_tensor(out=sum1[:], in0=twos[:, :, 0], in1=twos[:, :, 1], op=ADD)
+                nc.gpsimd.tensor_tensor(
+                    out=result_halves[:, :, 0:gpsimd_out],
+                    in0=sum1[:].rearrange("p (a o) -> p a o", a=HALVES_CHUNK),
+                    in1=terms[:, :, 0:gpsimd_out, 8],
+                    op=ADD,
+                )
             nc.sync.dma_start(
                 out=out_rows[c * CHUNK : (c + 1) * CHUNK, :].rearrange("(n p) o -> p n o", p=P),
                 in_=result[:].rearrange("p (n o) -> p n o", n=CHUNK_TILES),

@@ -42,7 +42,7 @@ P_HALF = TAPS * C_OUT // 2
 HALF_GROUPS = GROUPS // 2
 HALF_OUT = C_OUT // 2
 BANK_GROUPS = BANK // GROUP_LEN
-GPSIMD_OUT = 88
+GPSIMD_OUT = 72
 HALVES_CHUNK = 2 * CHUNK_TILES
 
 LOAD_AHEAD = 3
@@ -58,12 +58,13 @@ def tile_involution2d_pa_kernel(tc, x, Wi, bi, w_span, out):
     out_rows = out.rearrange("b u v o -> (b u v) o")
 
     with ExitStack() as ctx:
+        ctx.enter_context(tc.manual_schedule())
         const = ctx.enter_context(tc.tile_pool(name="const", bufs=1))
         x_pool = ctx.enter_context(tc.tile_pool(name="x", bufs=LOAD_AHEAD + 1))
         mx_pool = ctx.enter_context(tc.tile_pool(name="mx", bufs=2))
-        q_pool = ctx.enter_context(tc.tile_pool(name="q", bufs=3))
+        q_pool = ctx.enter_context(tc.tile_pool(name="q", bufs=2))
         sum_pool = ctx.enter_context(tc.tile_pool(name="sums", bufs=1))
-        out_pool = ctx.enter_context(tc.tile_pool(name="out", bufs=3))
+        out_pool = ctx.enter_context(tc.tile_pool(name="out", bufs=2))
         xt_psum = ctx.enter_context(tc.psum_pool(name="xt", bufs=2))
         xi_psum = ctx.enter_context(tc.psum_pool(name="xi", bufs=1))
         p_psum = ctx.enter_context(tc.psum_pool(name="p", bufs=5))
@@ -86,6 +87,9 @@ def tile_involution2d_pa_kernel(tc, x, Wi, bi, w_span, out):
             out=wi_raw[:].rearrange("p (s ec) -> p s ec", s=2 * PASSES),
             in_=Wi.rearrange("(s q e) c -> q s (e c)", q=P, e=2),
         )
+        bias_rows = const.tile([P, P], BF16, name="bias_rows")
+        nc.vector.memset(bias_rows[:], 0.0)
+        nc.sync.dma_start(out=bias_rows[0:C_HALVES, :], in_=bi.rearrange("(h c) -> h c", h=C_HALVES))
         for c in range(1, LOAD_AHEAD):
             load_x(c)
 
@@ -103,9 +107,6 @@ def tile_involution2d_pa_kernel(tc, x, Wi, bi, w_span, out):
         wi_scales = const.tile([P, PASSES * C_OUT], U8, name="wi_scales", align_bytes=64)
         nc.vector.quantize_mx(out=wi_codes[:].bitcast(FP8X4), scales=wi_scales[:], in_=wi_grouped[:])
 
-        bias_rows = const.tile([P, P], BF16, name="bias_rows")
-        nc.vector.memset(bias_rows[:], 0.0)
-        nc.sync.dma_start(out=bias_rows[0:C_HALVES, :], in_=bi.rearrange("(h c) -> h c", h=C_HALVES))
         bias_rows_f32 = const.tile([P, P], F32, name="bias_rows_f32")
         nc.vector.tensor_copy(out=bias_rows_f32[:], in_=bias_rows[:])
         bias_ps = xt_psum.tile([P, P], F32, name="bias_ps", tag="xt")
@@ -192,7 +193,7 @@ def tile_involution2d_pa_kernel(tc, x, Wi, bi, w_span, out):
                         scale=1.0,
                     )
 
-        def involve(c):
+        def involve(c, to_quantise):
             b = c // CHUNKS_IMAGE
             q = q_pool.tile([P, HALVES_CHUNK * P_HALF], F32, name="q")
             for n in range(CHUNK_TILES):
@@ -216,6 +217,8 @@ def tile_involution2d_pa_kernel(tc, x, Wi, bi, w_span, out):
                                 ),
                                 shifter[:, shift : shift + P],
                             )
+                        if (n, half, g0) == (CHUNK_TILES - 1, 1, 0) and to_quantise < CHUNKS:
+                            quantise_x(to_quantise)
                         w_first = (half * HALF_GROUPS + g0) * TAPS
                         at = (n * 2 + half) * P_HALF + g0 * GROUP_LEN
                         nc.vector.tensor_tensor(
@@ -276,11 +279,11 @@ def tile_involution2d_pa_kernel(tc, x, Wi, bi, w_span, out):
         for step in range(CHUNKS + INVOLVE_LAG):
             if step + LOAD_AHEAD < CHUNKS:
                 load_x(step + LOAD_AHEAD)
-            if step < CHUNKS:
-                transpose_x(step)
-            if 0 <= step - QUANTISE_LAG < CHUNKS:
-                quantise_x(step - QUANTISE_LAG)
             if 0 <= step - PROJECT_LAG < CHUNKS:
                 project(step - PROJECT_LAG)
             if step >= INVOLVE_LAG:
-                involve(step - INVOLVE_LAG)
+                involve(step - INVOLVE_LAG, step - QUANTISE_LAG)
+            elif step >= QUANTISE_LAG:
+                quantise_x(step - QUANTISE_LAG)
+            if step < CHUNKS:
+                transpose_x(step)

from contextlib import ExitStack

import concourse.mybir as mybir
from concourse.masks import make_identity

F32 = mybir.dt.float32
BF16 = mybir.dt.bfloat16
U32 = mybir.dt.uint32
U8 = mybir.dt.uint8
FP8X4 = mybir.dt.float8_e4m3fn_x4
MULT = mybir.AluOpType.mult
ADD = mybir.AluOpType.add

P = 128

IMAGES, HEIGHT, WIDTH = 4, 32, 32
C_IN, C_OUT = 1024, 256
WINDOW = 3
TAPS = WINDOW * WINDOW
GROUPS = 16
GROUP_CHANNELS = C_OUT // GROUPS
GROUP_LEN = GROUP_CHANNELS * TAPS
PIXELS = IMAGES * HEIGHT * WIDTH

FLOPS = 2 * PIXELS * C_IN * C_OUT + 2 * PIXELS * TAPS * C_OUT

K_PASS = 4 * P
PASSES = C_IN // K_PASS
WORDS_PASS = K_PASS // 2
C_HALVES = C_OUT // P
CHUNK = 256
CHUNK_TILES = CHUNK // P
CHUNK_ROWS = CHUNK // WIDTH
CHUNKS = PIXELS // CHUNK
CHUNKS_IMAGE = HEIGHT // CHUNK_ROWS
PADDED_ROWS = HEIGHT + 2
BLOCK_F32 = 8

TILE_ROWS = P // WIDTH
BANK = 512
P_HALF = TAPS * C_OUT // 2
HALF_GROUPS = GROUPS // 2
HALF_OUT = C_OUT // 2
BANK_GROUPS = BANK // GROUP_LEN
GPSIMD_OUT = 72
HALVES_CHUNK = 2 * CHUNK_TILES

LOAD_AHEAD = 3
QUANTISE_LAG = 1
PROJECT_LAG = 2
INVOLVE_LAG = 3


def tile_involution2d_pa_kernel(tc, x, Wi, bi, w_span, out):
    nc = tc.nc
    x_rows = x.rearrange("b u v k -> (b u v) k")
    w_rows = w_span.rearrange("b u v c -> (b u v) c")
    out_rows = out.rearrange("b u v o -> (b u v) o")

    with ExitStack() as ctx:
        ctx.enter_context(tc.manual_schedule())
        const = ctx.enter_context(tc.tile_pool(name="const", bufs=1))
        x_pool = ctx.enter_context(tc.tile_pool(name="x", bufs=LOAD_AHEAD + 1))
        mx_pool = ctx.enter_context(tc.tile_pool(name="mx", bufs=2))
        q_pool = ctx.enter_context(tc.tile_pool(name="q", bufs=2))
        sum_pool = ctx.enter_context(tc.tile_pool(name="sums", bufs=1))
        out_pool = ctx.enter_context(tc.tile_pool(name="out", bufs=2))
        xt_psum = ctx.enter_context(tc.psum_pool(name="xt", bufs=2))
        xi_psum = ctx.enter_context(tc.psum_pool(name="xi", bufs=1))
        p_psum = ctx.enter_context(tc.psum_pool(name="p", bufs=5))

        x_tiles = {}
        grouped_tiles = {}
        code_tiles = {}

        def load_x(c):
            x_sb = x_pool.tile([P, CHUNK_TILES * C_IN], BF16, name="x_sb")
            nc.sync.dma_start(
                out=x_sb[:].rearrange("p (n k) -> p n k", n=CHUNK_TILES),
                in_=x_rows[c * CHUNK : (c + 1) * CHUNK, :].rearrange("(n p) k -> p n k", p=P),
            )
            x_tiles[c] = x_sb

        load_x(0)
        wi_raw = const.tile([P, PASSES * 4 * C_OUT], BF16, name="wi_raw")
        nc.sync.dma_start(
            out=wi_raw[:].rearrange("p (s ec) -> p s ec", s=2 * PASSES),
            in_=Wi.rearrange("(s q e) c -> q s (e c)", q=P, e=2),
        )
        bias_rows = const.tile([P, P], BF16, name="bias_rows")
        nc.vector.memset(bias_rows[:], 0.0)
        nc.sync.dma_start(out=bias_rows[0:C_HALVES, :], in_=bi.rearrange("(h c) -> h c", h=C_HALVES))
        for c in range(1, LOAD_AHEAD):
            load_x(c)

        shifter = const.tile([P, 2 * P], F32, name="shifter")
        make_identity(nc, shifter[:, 0:P])
        nc.gpsimd.memset(shifter[:, P : 2 * P], 0.0)
        identity = shifter[:, 0:P]

        wi_grouped = const.tile([P, PASSES * C_OUT * 4], BF16, name="wi_grouped", align_bytes=64)
        nc.vector.tensor_copy(
            out=wi_grouped[:].rearrange("p (g c t) -> p g c t", g=PASSES, t=4),
            in_=wi_raw[:].rearrange("p (g t c) -> p g c t", g=PASSES, t=4),
        )
        wi_codes = const.tile([P, PASSES * C_OUT], U32, name="wi_codes", align_bytes=64)
        wi_scales = const.tile([P, PASSES * C_OUT], U8, name="wi_scales", align_bytes=64)
        nc.vector.quantize_mx(out=wi_codes[:].bitcast(FP8X4), scales=wi_scales[:], in_=wi_grouped[:])

        bias_rows_f32 = const.tile([P, P], F32, name="bias_rows_f32")
        nc.vector.tensor_copy(out=bias_rows_f32[:], in_=bias_rows[:])
        bias_ps = xt_psum.tile([P, P], F32, name="bias_ps", tag="xt")
        nc.tensor.transpose(bias_ps[:], bias_rows_f32[:], identity)
        bias_cols = const.tile([P, C_HALVES], F32, name="bias_cols")
        nc.vector.tensor_copy(out=bias_cols[:], in_=bias_ps[:, 0:C_HALVES])

        w_sb = const.tile([P, (PIXELS // P) * GROUPS * TAPS], BF16, name="w_sb")
        w_tiles = w_sb[:].rearrange("p (n c) -> p n c", c=GROUPS * TAPS)
        tiles_image = HEIGHT // TILE_ROWS
        for b in range(IMAGES):
            nc.sync.dma_start(
                out=w_tiles[:, b * tiles_image : (b + 1) * tiles_image, :],
                in_=w_rows[b * HEIGHT * WIDTH : (b + 1) * HEIGHT * WIDTH, :].rearrange(
                    "(n p) c -> p n c", p=P
                ),
            )

        shifted = []
        for j in range(WINDOW):
            xi_sb = const.tile([P, C_HALVES * IMAGES * PADDED_ROWS * WIDTH], F32, name="xi_sb%d" % j)
            view = xi_sb[:].rearrange(
                "p (h b r v) -> p h b r v", h=C_HALVES, b=IMAGES, r=PADDED_ROWS
            )
            nc.gpsimd.memset(view[:, :, :, 0, :], 0.0)
            nc.gpsimd.memset(view[:, :, :, PADDED_ROWS - 1, :], 0.0)
            shifted.append(view)
        nc.gpsimd.memset(shifted[0][:, :, :, :, 0:BLOCK_F32], 0.0)
        nc.gpsimd.memset(shifted[WINDOW - 1][:, :, :, :, WIDTH - BLOCK_F32 : WIDTH], 0.0)

        def transpose_x(c):
            x_words = x_tiles[c][:].bitcast(F32)
            grouped = mx_pool.tile([P, PASSES * CHUNK * 4], BF16, name="grouped", align_bytes=64)
            grouped_words = grouped[:].bitcast(F32).rearrange(
                "p (g r u) -> p g r u", g=PASSES, u=2
            )
            for n in range(CHUNK_TILES):
                xt = xt_psum.tile([P, 2 * PASSES, P], F32, name="xt", tag="xt")
                for s in range(2 * PASSES):
                    first = n * (C_IN // 2) + s * P
                    nc.tensor.transpose(xt[:, s, :], x_words[:, first : first + P], identity)
                nc.scalar.copy(
                    out=grouped_words[:, :, n * P : (n + 1) * P, :],
                    in_=xt[:].rearrange("p (g u) r -> p g r u", u=2),
                )
            grouped_tiles[c] = grouped

        def quantise_x(c):
            codes = mx_pool.tile([P, PASSES * CHUNK], U32, name="codes", align_bytes=64)
            scales = mx_pool.tile([P, PASSES * CHUNK], U8, name="scales", align_bytes=64)
            nc.vector.quantize_mx(
                out=codes[:].bitcast(FP8X4), scales=scales[:], in_=grouped_tiles[c][:]
            )
            code_tiles[c] = (codes, scales)

        def project(c):
            codes, scales = code_tiles[c]
            xi_ps = xi_psum.tile([P, C_HALVES, CHUNK], F32, name="xi_ps")
            for h in range(C_HALVES):
                for g in range(PASSES):
                    wi_cols = slice(g * C_OUT + h * P, g * C_OUT + (h + 1) * P)
                    x_cols = slice(g * CHUNK, (g + 1) * CHUNK)
                    nc.tensor.matmul_mx(
                        out=xi_ps[:, h, :],
                        lhsT=wi_codes[:, wi_cols].bitcast(FP8X4),
                        lhsT_scale=wi_scales[:, wi_cols],
                        rhs=codes[:, x_cols].bitcast(FP8X4),
                        rhs_scale=scales[:, x_cols],
                        start=(g == 0),
                        stop=(g == PASSES - 1),
                    )
            b = c // CHUNKS_IMAGE
            first_row = 1 + (c % CHUNKS_IMAGE) * CHUNK_ROWS
            for h in range(C_HALVES):
                xi_rows = xi_ps[:, h, :].rearrange("p (r v) -> p r v", v=WIDTH)
                for j in range(WINDOW):
                    lo = max(0, 1 - j)
                    hi = min(WIDTH, WIDTH + 1 - j)
                    nc.scalar.activation(
                        out=shifted[j][:, h, b, first_row : first_row + CHUNK_ROWS, lo:hi],
                        in_=xi_rows[:, :, lo + j - 1 : hi + j - 1],
                        func=mybir.ActivationFunctionType.Identity,
                        bias=bias_cols[:, h : h + 1],
                        scale=1.0,
                    )

        def involve(c, to_quantise):
            b = c // CHUNKS_IMAGE
            q = q_pool.tile([P, HALVES_CHUNK * P_HALF], F32, name="q")
            for n in range(CHUNK_TILES):
                tile_index = c * CHUNK_TILES + n
                top = (c % CHUNKS_IMAGE) * CHUNK_ROWS + n * TILE_ROWS
                for half in range(2):
                    for g0 in reversed(range(0, HALF_GROUPS, BANK_GROUPS)):
                        groups = min(BANK_GROUPS, HALF_GROUPS - g0)
                        first = half * P_HALF + g0 * GROUP_LEN
                        last = first + groups * GROUP_LEN
                        p_ps = p_psum.tile([P, BANK], F32, name="p_ps")
                        for block in range(first // P, (last + P - 1) // P):
                            t, h = block // C_HALVES, block % C_HALVES
                            i, j = t // WINDOW, t % WINDOW
                            column = max(0, block * P - first)
                            shift = max(0, first - block * P)
                            nc.tensor.transpose(
                                p_ps[:, column : column + P],
                                shifted[j][:, h, b, top + i : top + i + TILE_ROWS, :].rearrange(
                                    "p r v -> p (r v)"
                                ),
                                shifter[:, shift : shift + P],
                            )
                        if (n, half, g0) == (CHUNK_TILES - 1, 1, 0) and to_quantise < CHUNKS:
                            quantise_x(to_quantise)
                        w_first = (half * HALF_GROUPS + g0) * TAPS
                        at = (n * 2 + half) * P_HALF + g0 * GROUP_LEN
                        nc.vector.tensor_tensor(
                            out=q[:, at : at + groups * GROUP_LEN].rearrange(
                                "p (g c m) -> p g c m", c=GROUP_CHANNELS, m=TAPS
                            ),
                            in0=p_ps[:, 0 : groups * GROUP_LEN].rearrange(
                                "p (g c m) -> p g c m", c=GROUP_CHANNELS, m=TAPS
                            ),
                            in1=w_tiles[:, tile_index, w_first : w_first + groups * TAPS]
                            .rearrange("p (g m) -> p g m", m=TAPS)
                            .unsqueeze(2)
                            .to_broadcast([P, groups, GROUP_CHANNELS, TAPS]),
                            op=MULT,
                        )

            gpsimd_out = GPSIMD_OUT if c < CHUNKS - 1 else 0
            terms = q[:].rearrange("p (a o m) -> p a o m", a=HALVES_CHUNK, m=TAPS)
            result = out_pool.tile([P, HALVES_CHUNK * HALF_OUT], F32, name="result")
            result_halves = result[:].rearrange("p (a o) -> p a o", a=HALVES_CHUNK)
            nc.vector.tensor_reduce(
                out=result_halves[:, :, gpsimd_out:HALF_OUT],
                in_=terms[:, :, gpsimd_out:HALF_OUT, :],
                axis=mybir.AxisListType.X,
                op=ADD,
            )
            if gpsimd_out > 0:
                count = HALVES_CHUNK * gpsimd_out
                sum4 = sum_pool.tile([P, count * 4], F32, name="sum4")
                sum2 = sum_pool.tile([P, count * 2], F32, name="sum2")
                sum1 = sum_pool.tile([P, count], F32, name="sum1")
                nc.gpsimd.tensor_tensor(
                    out=sum4[:].rearrange("p (a o m) -> p a o m", a=HALVES_CHUNK, m=4),
                    in0=terms[:, :, 0:gpsimd_out, 0:4],
                    in1=terms[:, :, 0:gpsimd_out, 4:8],
                    op=ADD,
                )
                fours = sum4[:].rearrange("p (o m) -> p o m", m=4)
                nc.gpsimd.tensor_tensor(
                    out=sum2[:].rearrange("p (o m) -> p o m", m=2),
                    in0=fours[:, :, 0:2],
                    in1=fours[:, :, 2:4],
                    op=ADD,
                )
                twos = sum2[:].rearrange("p (o m) -> p o m", m=2)
                nc.gpsimd.tensor_tensor(out=sum1[:], in0=twos[:, :, 0], in1=twos[:, :, 1], op=ADD)
                nc.gpsimd.tensor_tensor(
                    out=result_halves[:, :, 0:gpsimd_out],
                    in0=sum1[:].rearrange("p (a o) -> p a o", a=HALVES_CHUNK),
                    in1=terms[:, :, 0:gpsimd_out, 8],
                    op=ADD,
                )
            nc.sync.dma_start(
                out=out_rows[c * CHUNK : (c + 1) * CHUNK, :].rearrange("(n p) o -> p n o", p=P),
                in_=result[:].rearrange("p (n o) -> p n o", n=CHUNK_TILES),
            )

        for step in range(CHUNKS + INVOLVE_LAG):
            if step + LOAD_AHEAD < CHUNKS:
                load_x(step + LOAD_AHEAD)
            if 0 <= step - PROJECT_LAG < CHUNKS:
                project(step - PROJECT_LAG)
            if step >= INVOLVE_LAG:
                involve(step - INVOLVE_LAG, step - QUANTISE_LAG)
            elif step >= QUANTISE_LAG:
                quantise_x(step - QUANTISE_LAG)
            if step < CHUNKS:
                transpose_x(step)
